import numpy as np
import ml_dtypes


def mxq(x, axis, fmt="e4m3"):
    dtype, down = {"e4m3": (ml_dtypes.float8_e4m3fn, 7), "e5m2": (ml_dtypes.float8_e5m2, 14)}[fmt]
    v = np.moveaxis(np.asarray(x, np.float32).astype(ml_dtypes.bfloat16).astype(np.float64), axis, -1)
    blocks = v.reshape(v.shape[:-1] + (-1, 32))
    amax = np.abs(blocks).max(-1, keepdims=True)
    byte = np.maximum(np.where(amax > 0, np.frexp(amax)[1] - 1 + 127, 0) - down, 1)
    scale = np.exp2(byte - 127.0)
    codes = (blocks / scale).astype(np.float32).astype(dtype).astype(np.float64)
    return np.moveaxis((codes * scale).reshape(v.shape), -1, axis)


WIDE = False


def mx_kscale(k):
    if not WIDE:
        return np.ones(k)
    levels = np.array([10, -10, 5, -5, 0])
    a = np.random.permutation(np.resize(levels, k // 512 * 4)).reshape(k // 512, 4)
    idx = np.arange(k)
    return np.exp2(a[idx // 512, idx % 128 // 32])


BF16 = ml_dtypes.bfloat16


def bf(x):
    return np.asarray(x, np.float32).astype(BF16)


def f64(x):
    return np.asarray(x).astype(np.float64)


B, L, D_MODEL, N_HEADS = 2, 512, 1024, 16
HEAD_DIM = D_MODEL // N_HEADS


def apply_rope(x, cos, sin):
    xr = x.reshape(x.shape[:-1] + (HEAD_DIM // 2, 2))
    xe, xo = xr[..., 0], xr[..., 1]
    c = cos[None, :, None, :]
    s = sin[None, :, None, :]
    oe = xe * c - xo * s
    oo = xe * s + xo * c
    return np.stack([oe, oo], axis=-1).reshape(x.shape)


def setup_inputs():
    s = mx_kscale(D_MODEL)
    inv_freq = 1.0 / (10000.0 ** (np.arange(0, HEAD_DIM, 2) / HEAD_DIM))
    angles = np.outer(np.arange(L), inv_freq)
    return {"hidden_states": bf(np.random.standard_normal((B, L, D_MODEL)) * s),
            "w_qkv": bf(np.random.standard_normal((3 * D_MODEL, D_MODEL)) / np.sqrt(D_MODEL) / s[None, :]),
            "freqs_cos": bf(np.cos(angles)),
            "freqs_sin": bf(np.sin(angles))}


def reference(hidden_states, w_qkv, freqs_cos, freqs_sin):
    qkv = mxq(f64(hidden_states), 2, "e4m3") @ mxq(f64(w_qkv), 1, "e4m3").T
    xq, xk, xv = np.split(qkv, 3, axis=-1)
    xq = xq.reshape(B, L, N_HEADS, HEAD_DIM)
    xk = xk.reshape(B, L, N_HEADS, HEAD_DIM)
    xv = xv.reshape(B, L, N_HEADS, HEAD_DIM)
    xq = apply_rope(xq, f64(freqs_cos), f64(freqs_sin))
    xk = apply_rope(xk, f64(freqs_cos), f64(freqs_sin))
    q = xq.transpose(0, 2, 1, 3)
    k = xk.transpose(0, 2, 1, 3)
    v = xv.transpose(0, 2, 1, 3)
    return q, k, v

@@ -1,0 +1,170 @@
+from contextlib import ExitStack
+
+import concourse.mybir as mybir
+from concourse.masks import make_identity
+
+BF16 = mybir.dt.bfloat16
+F32 = mybir.dt.float32
+U32 = mybir.dt.uint32
+U8 = mybir.dt.uint8
+FP8X4 = mybir.dt.float8_e4m3fn_x4
+MULT = mybir.AluOpType.mult
+ADD = mybir.AluOpType.add
+
+P = 128
+BATCH = 2
+POSITIONS = 512
+K = 1024
+HEAD = 64
+PAIRS = HEAD // 2
+TILES = POSITIONS // P
+PACK = 4
+PASSES = K // (P * PACK)
+N = 512
+HEADS_N = N // HEAD
+HALVES = 1024 // N
+ROW_WORDS = K // 2
+PASS_WORDS = ROW_WORDS // PASSES
+OPERAND_COLS = 1024
+Q, KEY, V = 0, 1, 2
+PART_ORDER = (Q, V, KEY)
+
+FLOPS = 2 * BATCH * POSITIONS * K * 3072
+
+
+def tile_bertselfattention_pa_kernel(
+    tc, hidden_states, w_qkv, freqs_cos, freqs_sin, out_0, out_1, out_2
+):
+    nc = tc.nc
+    outputs = (out_0, out_1, out_2)
+
+    with ExitStack() as stack:
+        keep = stack.enter_context(tc.tile_pool(name="keep", bufs=1))
+        stage = stack.enter_context(tc.tile_pool(name="stage", bufs=2))
+        work = stack.enter_context(tc.tile_pool(name="work", bufs=4))
+        results = stack.enter_context(tc.tile_pool(name="results", bufs=4))
+        turned_banks = stack.enter_context(tc.psum_pool(name="turned_banks", bufs=4))
+        sum_banks = stack.enter_context(tc.psum_pool(name="sum_banks", bufs=4))
+
+        def load_tokens(b):
+            rows = keep.tile([P, TILES * K], BF16, name="x_rows%d" % b)
+            nc.sync.dma_start(out=rows[:], in_=hidden_states[b].rearrange("(p t) k -> p (t k)", t=TILES))
+            return rows
+
+        def load_weights(part, half):
+            first = part * 1024 + half * N
+            rows = keep.tile([P, TILES * K], BF16, name="w_rows%d%d" % (part, half))
+            nc.sync.dma_start(
+                out=rows[:].rearrange("p (n ek) -> p n ek", n=2),
+                in_=w_qkv[first : first + N, :].rearrange("(n p e) k -> p n (e k)", n=2, e=2),
+            )
+            return rows
+
+        token_starts = [[t * ROW_WORDS + g * PASS_WORDS for g in range(PASSES)] for t in range(TILES)]
+        weight_starts = [
+            [(2 * n + e) * ROW_WORDS + g * PASS_WORDS for n in range(2)]
+            for g in range(PASSES)
+            for e in range(2)
+        ]
+
+        jobs = []
+        for half in range(HALVES):
+            jobs.append((("x", half), load_tokens(half), token_starts))
+            for part in PART_ORDER:
+                jobs.append(((part, half), load_weights(part, half), weight_starts))
+
+        cos_rows = keep.tile([P, TILES, PAIRS], BF16, name="cos_rows")
+        sin_rows = keep.tile([P, TILES, PAIRS], BF16, name="sin_rows")
+        nc.scalar.dma_start(out=cos_rows[:], in_=freqs_cos.rearrange("(p t) j -> p t j", t=TILES))
+        nc.scalar.dma_start(out=sin_rows[:], in_=freqs_sin.rearrange("(p t) j -> p t j", t=TILES))
+
+        identity = keep.tile([P, P], F32, name="identity")
+        make_identity(nc, identity[:])
+
+        factors = keep.tile([P, TILES, 2, N], F32, name="factors")
+        factor_view = factors[:].rearrange("p t r (e h j) -> p t r e h j", e=2, h=HEADS_N)
+        rotation = ((0, 0, cos_rows, 1.0), (0, 1, sin_rows, -1.0), (1, 0, sin_rows, 1.0), (1, 1, cos_rows, 1.0))
+        for r, e, rows, sign in rotation:
+            nc.gpsimd.tensor_scalar(
+                out=factor_view[:, :, r, e],
+                in0=rows[:].unsqueeze(2).to_broadcast([P, TILES, HEADS_N, PAIRS]),
+                scalar1=sign,
+                scalar2=0.0,
+                op0=MULT,
+                op1=ADD,
+            )
+
+        def turn(rows, starts):
+            words = rows[:].bitcast(F32)
+            grouped = stage.tile([P, OPERAND_COLS * PACK], BF16, align_bytes=64, name="grouped")
+            grouped_words = grouped[:].bitcast(F32).rearrange("p (i c u) -> p i c u", c=2 * P, u=2)
+            for i, bank_starts in enumerate(starts):
+                turned = turned_banks.tile([P, 2, 2 * P], F32, name="turned")
+                for c, start in enumerate(bank_starts):
+                    for u in range(2):
+                        nc.tensor.transpose(
+                            turned[:, u, c * P : (c + 1) * P],
+                            words[:, start + u * P : start + (u + 1) * P],
+                            identity[:],
+                        )
+                nc.scalar.copy(out=grouped_words[:, i], in_=turned[:].rearrange("p u c -> p c u"))
+            return grouped
+
+        def quantise(key, grouped):
+            codes = keep.tile([P, OPERAND_COLS], U32, align_bytes=64, name="codes_%s%d" % key)
+            scales = keep.tile([P, OPERAND_COLS], U8, align_bytes=64, name="scales_%s%d" % key)
+            nc.vector.quantize_mx(out=codes[:].bitcast(FP8X4), scales=scales[:], in_=grouped[:])
+            return codes, scales
+
+        ready = {}
+
+        for key, rows, starts in jobs[:2]:
+            ready[key] = quantise(key, turn(rows, starts))
+        step = 0
+
+        for half in range(HALVES):
+            for b in range(BATCH):
+                for part in PART_ORDER:
+                    ahead = jobs[step + 2] if step + 2 < len(jobs) else None
+                    step += 1
+                    grouped_ahead = turn(ahead[1], ahead[2]) if ahead else None
+
+                    x_codes, x_scales = ready[("x", b)]
+                    w_codes, w_scales = ready[(part, half)]
+                    result = results.tile([P, HEADS_N, TILES, HEAD], F32, name="result")
+                    for t in range(TILES):
+                        if ahead and t == TILES // 2:
+                            ready[ahead[0]] = quantise(ahead[0], grouped_ahead)
+                        sums = sum_banks.tile([P, N], F32, name="sums")
+                        for g in range(PASSES):
+                            tokens = slice((t * PASSES + g) * P, (t * PASSES + g + 1) * P)
+                            columns = slice(g * N, (g + 1) * N)
+                            nc.tensor.matmul_mx(
+                                out=sums[:],
+                                lhsT=x_codes[:, tokens].bitcast(FP8X4),
+                                lhsT_scale=x_scales[:, tokens],
+                                rhs=w_codes[:, columns].bitcast(FP8X4),
+                                rhs_scale=w_scales[:, columns],
+                                start=(g == 0),
+                                stop=(g == PASSES - 1),
+                            )
+                        natural = result[:, :, t, :].rearrange("p h (j r) -> p h j r", r=2)
+                        if part == V:
+                            nc.scalar.copy(
+                                out=natural, in_=sums[:].rearrange("p (r h j) -> p h j r", r=2, h=HEADS_N)
+                            )
+                        else:
+                            products = work.tile([P, 2, N], F32, name="products")
+                            nc.vector.tensor_tensor(
+                                out=products[:],
+                                in0=sums[:].unsqueeze(1).to_broadcast([P, 2, N]),
+                                in1=factors[:, t],
+                                op=MULT,
+                            )
+                            terms = products[:].rearrange("p r (e h j) -> p e h j r", e=2, h=HEADS_N)
+                            nc.gpsimd.tensor_tensor(out=natural, in0=terms[:, 0], in1=terms[:, 1], op=ADD)
+                    heads = slice(half * HEADS_N, (half + 1) * HEADS_N)
+                    nc.sync.dma_start(
+                        out=outputs[part][b, heads].rearrange("h (p t) d -> p h (t d)", t=TILES),
+                        in_=result[:].rearrange("p h t d -> p h (t d)"),
+                    )

@@ -81,17 +81,11 @@ def tile_bertselfattention_pa_kernel(
         identity = keep.tile([P, P], F32, name="identity")
         make_identity(nc, identity[:])
 
-        factors = keep.tile([P, TILES, 2, N], F32, name="factors")
-        factor_view = factors[:].rearrange("p t r (e h j) -> p t r e h j", e=2, h=HEADS_N)
+        factors = keep.tile([P, TILES, 2, PAIRS, 2], F32, name="factors")
         rotation = ((0, 0, cos_rows, 1.0), (0, 1, sin_rows, -1.0), (1, 0, sin_rows, 1.0), (1, 1, cos_rows, 1.0))
         for r, e, rows, sign in rotation:
             nc.gpsimd.tensor_scalar(
-                out=factor_view[:, :, r, e],
-                in0=rows[:].unsqueeze(2).to_broadcast([P, TILES, HEADS_N, PAIRS]),
-                scalar1=sign,
-                scalar2=0.0,
-                op0=MULT,
-                op1=ADD,
+                out=factors[:, :, e, :, r], in0=rows[:], scalar1=sign, scalar2=0.0, op0=MULT, op1=ADD
             )
 
         def turn(rows, starts):
@@ -148,21 +142,25 @@ def tile_bertselfattention_pa_kernel(
                                 start=(g == 0),
                                 stop=(g == PASSES - 1),
                             )
-                        natural = result[:, :, t, :].rearrange("p h (j r) -> p h j r", r=2)
                         if part == V:
                             nc.scalar.copy(
-                                out=natural, in_=sums[:].rearrange("p (r h j) -> p h j r", r=2, h=HEADS_N)
+                                out=result[:, :, t, :].rearrange("p h (j r) -> p h j r", r=2),
+                                in_=sums[:].rearrange("p (r h j) -> p h j r", r=2, h=HEADS_N),
                             )
                         else:
-                            products = work.tile([P, 2, N], F32, name="products")
+                            products = work.tile([P, 2, HEADS_N, HEAD], F32, name="products")
                             nc.vector.tensor_tensor(
-                                out=products[:],
-                                in0=sums[:].unsqueeze(1).to_broadcast([P, 2, N]),
-                                in1=factors[:, t],
+                                out=products[:].rearrange("p e h (j r) -> p e h j r", r=2),
+                                in0=sums[:]
+                                .rearrange("p (e h j) -> p e h j", e=2, h=HEADS_N)
+                                .unsqueeze(4)
+                                .to_broadcast([P, 2, HEADS_N, PAIRS, 2]),
+                                in1=factors[:, t].unsqueeze(2).to_broadcast([P, 2, HEADS_N, PAIRS, 2]),
                                 op=MULT,
                             )
-                            terms = products[:].rearrange("p r (e h j) -> p e h j r", e=2, h=HEADS_N)
-                            nc.gpsimd.tensor_tensor(out=natural, in0=terms[:, 0], in1=terms[:, 1], op=ADD)
+                            nc.gpsimd.tensor_tensor(
+                                out=result[:, :, t, :], in0=products[:, 0], in1=products[:, 1], op=ADD
+                            )
                     heads = slice(half * HEADS_N, (half + 1) * HEADS_N)
                     nc.sync.dma_start(
                         out=outputs[part][b, heads].rearrange("h (p t) d -> p h (t d)", t=TILES),

@@ -18,16 +18,15 @@ K = 1024
 HEAD = 64
 PAIRS = HEAD // 2
 TILES = POSITIONS // P
-PACK = 4
-PASSES = K // (P * PACK)
-N = 512
-HEADS_N = N // HEAD
-HALVES = 1024 // N
+PASSES = K // (P * 4)
+ROWS = 2 * P
 ROW_WORDS = K // 2
 PASS_WORDS = ROW_WORDS // PASSES
-OPERAND_COLS = 1024
+CHUNK_COLS = PASSES * ROWS
+CHUNK_HEADS = ROWS // HEAD
+PAIR_HEADS = 2 * CHUNK_HEADS
+N = 2 * ROWS
 Q, KEY, V = 0, 1, 2
-PART_ORDER = (Q, V, KEY)
 
 FLOPS = 2 * BATCH * POSITIONS * K * 3072
 
@@ -40,38 +39,30 @@ def tile_bertselfattention_pa_kernel(
 
     with ExitStack() as stack:
         keep = stack.enter_context(tc.tile_pool(name="keep", bufs=1))
-        stage = stack.enter_context(tc.tile_pool(name="stage", bufs=2))
+        stage = stack.enter_context(tc.tile_pool(name="stage", bufs=4))
         work = stack.enter_context(tc.tile_pool(name="work", bufs=4))
-        results = stack.enter_context(tc.tile_pool(name="results", bufs=4))
+        results = stack.enter_context(tc.tile_pool(name="results", bufs=6))
         turned_banks = stack.enter_context(tc.psum_pool(name="turned_banks", bufs=4))
         sum_banks = stack.enter_context(tc.psum_pool(name="sum_banks", bufs=4))
 
-        def load_tokens(b):
-            rows = keep.tile([P, TILES * K], BF16, name="x_rows%d" % b)
-            nc.sync.dma_start(out=rows[:], in_=hidden_states[b].rearrange("(p t) k -> p (t k)", t=TILES))
-            return rows
+        chunk_rows = {}
 
-        def load_weights(part, half):
-            first = part * 1024 + half * N
-            rows = keep.tile([P, TILES * K], BF16, name="w_rows%d%d" % (part, half))
-            nc.sync.dma_start(
-                out=rows[:].rearrange("p (n ek) -> p n ek", n=2),
-                in_=w_qkv[first : first + N, :].rearrange("(n p e) k -> p n (e k)", n=2, e=2),
-            )
-            return rows
+        def load(key):
+            rows = keep.tile([P, 2 * K], BF16, name="rows_%s%d%d" % key)
+            name, i, c = key
+            if name == "x":
+                source = hidden_states[i].rearrange("(p t) k -> p t k", t=TILES)[:, 2 * c : 2 * c + 2, :]
+            else:
+                first = name * 1024 + (2 * i + c) * ROWS
+                source = w_qkv[first : first + ROWS, :].rearrange("(p e) k -> p e k", e=2)
+            nc.sync.dma_start(out=rows[:].rearrange("p (e k) -> p e k", e=2), in_=source)
+            chunk_rows[key] = rows
 
-        token_starts = [[t * ROW_WORDS + g * PASS_WORDS for g in range(PASSES)] for t in range(TILES)]
-        weight_starts = [
-            [(2 * n + e) * ROW_WORDS + g * PASS_WORDS for n in range(2)]
-            for g in range(PASSES)
-            for e in range(2)
-        ]
-
-        jobs = []
-        for half in range(HALVES):
-            jobs.append((("x", half), load_tokens(half), token_starts))
-            for part in PART_ORDER:
-                jobs.append(((part, half), load_weights(part, half), weight_starts))
+        for key in (("x", 0, 0), (Q, 0, 0), (Q, 0, 1), ("x", 0, 1), ("x", 1, 0), ("x", 1, 1)):
+            load(key)
+        for part, half in ((KEY, 0), (V, 0), (Q, 1), (V, 1), (KEY, 1)):
+            load((part, half, 0))
+            load((part, half, 1))
 
         cos_rows = keep.tile([P, TILES, PAIRS], BF16, name="cos_rows")
         sin_rows = keep.tile([P, TILES, PAIRS], BF16, name="sin_rows")
@@ -81,88 +72,127 @@ def tile_bertselfattention_pa_kernel(
         identity = keep.tile([P, P], F32, name="identity")
         make_identity(nc, identity[:])
 
-        factors = keep.tile([P, TILES, 2, PAIRS, 2], F32, name="factors")
+        factors = keep.tile([P, TILES, 2, CHUNK_HEADS, PAIRS, 2], F32, name="factors")
         rotation = ((0, 0, cos_rows, 1.0), (0, 1, sin_rows, -1.0), (1, 0, sin_rows, 1.0), (1, 1, cos_rows, 1.0))
         for r, e, rows, sign in rotation:
             nc.gpsimd.tensor_scalar(
-                out=factors[:, :, e, :, r], in0=rows[:], scalar1=sign, scalar2=0.0, op0=MULT, op1=ADD
+                out=factors[:, :, e, :, :, r],
+                in0=rows[:].unsqueeze(2).to_broadcast([P, TILES, CHUNK_HEADS, PAIRS]),
+                scalar1=sign,
+                scalar2=0.0,
+                op0=MULT,
+                op1=ADD,
             )
 
-        def turn(rows, starts):
-            words = rows[:].bitcast(F32)
-            grouped = stage.tile([P, OPERAND_COLS * PACK], BF16, align_bytes=64, name="grouped")
-            grouped_words = grouped[:].bitcast(F32).rearrange("p (i c u) -> p i c u", c=2 * P, u=2)
-            for i, bank_starts in enumerate(starts):
-                turned = turned_banks.tile([P, 2, 2 * P], F32, name="turned")
-                for c, start in enumerate(bank_starts):
-                    for u in range(2):
-                        nc.tensor.transpose(
-                            turned[:, u, c * P : (c + 1) * P],
-                            words[:, start + u * P : start + (u + 1) * P],
-                            identity[:],
-                        )
-                nc.scalar.copy(out=grouped_words[:, i], in_=turned[:].rearrange("p u c -> p c u"))
-            return grouped
-
-        def quantise(key, grouped):
-            codes = keep.tile([P, OPERAND_COLS], U32, align_bytes=64, name="codes_%s%d" % key)
-            scales = keep.tile([P, OPERAND_COLS], U8, align_bytes=64, name="scales_%s%d" % key)
-            nc.vector.quantize_mx(out=codes[:].bitcast(FP8X4), scales=scales[:], in_=grouped[:])
-            return codes, scales
-
+        grouped_chunks = {}
         ready = {}
 
-        for key, rows, starts in jobs[:2]:
-            ready[key] = quantise(key, turn(rows, starts))
-        step = 0
+        def turn(key, empty=nc.scalar.copy):
+            words = chunk_rows[key][:].bitcast(F32)
+            grouped = stage.tile([P, CHUNK_COLS * 4], BF16, align_bytes=64, name="grouped")
+            grouped_words = grouped[:].bitcast(F32).rearrange("p (i c u) -> p i c u", c=ROWS, u=2)
+            for i in range(2):
+                turned = turned_banks.tile([P, 2, ROWS], F32, name="turned")
+                for c in range(2):
+                    row, g = (i, c) if key[0] == "x" else (c, i)
+                    for u in range(2):
+                        start = row * ROW_WORDS + g * PASS_WORDS + u * P
+                        nc.tensor.transpose(
+                            turned[:, u, c * P : (c + 1) * P], words[:, start : start + P], identity[:]
+                        )
+                empty(out=grouped_words[:, i], in_=turned[:].rearrange("p u c -> p c u"))
+            grouped_chunks[key] = grouped
 
-        for half in range(HALVES):
-            for b in range(BATCH):
-                for part in PART_ORDER:
-                    ahead = jobs[step + 2] if step + 2 < len(jobs) else None
-                    step += 1
-                    grouped_ahead = turn(ahead[1], ahead[2]) if ahead else None
+        def quantise(key):
+            codes = keep.tile([P, CHUNK_COLS], U32, align_bytes=64, name="codes_%s%d%d" % key)
+            scales = keep.tile([P, CHUNK_COLS], U8, align_bytes=64, name="scales_%s%d%d" % key)
+            nc.vector.quantize_mx(out=codes[:].bitcast(FP8X4), scales=scales[:], in_=grouped_chunks[key][:])
+            ready[key] = (codes, scales)
 
-                    x_codes, x_scales = ready[("x", b)]
-                    w_codes, w_scales = ready[(part, half)]
-                    result = results.tile([P, HEADS_N, TILES, HEAD], F32, name="result")
-                    for t in range(TILES):
-                        if ahead and t == TILES // 2:
-                            ready[ahead[0]] = quantise(ahead[0], grouped_ahead)
-                        sums = sum_banks.tile([P, N], F32, name="sums")
-                        for g in range(PASSES):
-                            tokens = slice((t * PASSES + g) * P, (t * PASSES + g + 1) * P)
-                            columns = slice(g * N, (g + 1) * N)
-                            nc.tensor.matmul_mx(
-                                out=sums[:],
-                                lhsT=x_codes[:, tokens].bitcast(FP8X4),
-                                lhsT_scale=x_scales[:, tokens],
-                                rhs=w_codes[:, columns].bitcast(FP8X4),
-                                rhs_scale=w_scales[:, columns],
-                                start=(g == 0),
-                                stop=(g == PASSES - 1),
-                            )
-                        if part == V:
-                            nc.scalar.copy(
-                                out=result[:, :, t, :].rearrange("p h (j r) -> p h j r", r=2),
-                                in_=sums[:].rearrange("p (r h j) -> p h j r", r=2, h=HEADS_N),
-                            )
-                        else:
-                            products = work.tile([P, 2, HEADS_N, HEAD], F32, name="products")
-                            nc.vector.tensor_tensor(
-                                out=products[:].rearrange("p e h (j r) -> p e h j r", r=2),
-                                in0=sums[:]
-                                .rearrange("p (e h j) -> p e h j", e=2, h=HEADS_N)
-                                .unsqueeze(4)
-                                .to_broadcast([P, 2, HEADS_N, PAIRS, 2]),
-                                in1=factors[:, t].unsqueeze(2).to_broadcast([P, 2, HEADS_N, PAIRS, 2]),
-                                op=MULT,
-                            )
-                            nc.gpsimd.tensor_tensor(
-                                out=result[:, :, t, :], in0=products[:, 0], in1=products[:, 1], op=ADD
-                            )
-                    heads = slice(half * HEADS_N, (half + 1) * HEADS_N)
-                    nc.sync.dma_start(
-                        out=outputs[part][b, heads].rearrange("h (p t) d -> p h (t d)", t=TILES),
-                        in_=result[:].rearrange("p h t d -> p h (t d)"),
+        open_results = {}
+
+        def product(part, half, b, t):
+            x_codes, x_scales = ready[("x", b, t // 2)]
+            sums = sum_banks.tile([P, 2, ROWS], F32, name="sums")
+            for c in range(2):
+                w_codes, w_scales = ready[(part, half, c)]
+                for g in range(PASSES):
+                    tokens = slice(((t % 2) * PASSES + g) * P, ((t % 2) * PASSES + g + 1) * P)
+                    columns = slice(g * ROWS, (g + 1) * ROWS)
+                    nc.tensor.matmul_mx(
+                        out=sums[:, c],
+                        lhsT=x_codes[:, tokens].bitcast(FP8X4),
+                        lhsT_scale=x_scales[:, tokens],
+                        rhs=w_codes[:, columns].bitcast(FP8X4),
+                        rhs_scale=w_scales[:, columns],
+                        start=(g == 0),
+                        stop=(g == PASSES - 1),
                     )
+            if t == 0:
+                open_results[(part, half, b)] = results.tile([P, PAIR_HEADS, TILES, HEAD], F32, name="result")
+            result = open_results[(part, half, b)]
+            if part == V:
+                nc.scalar.copy(
+                    out=result[:, :, t, :].rearrange("p (c h) (j r) -> p c h j r", c=2, r=2),
+                    in_=sums[:].rearrange("p c (r h j) -> p c h j r", r=2, h=CHUNK_HEADS),
+                )
+            else:
+                products = work.tile([P, 2, 2, CHUNK_HEADS * HEAD], F32, name="products")
+                nc.vector.tensor_tensor(
+                    out=products[:].rearrange("p c e (m r) -> p c (e m) r", r=2),
+                    in0=sums[:].unsqueeze(3).to_broadcast([P, 2, ROWS, 2]),
+                    in1=factors[:, t]
+                    .rearrange("p e h j r -> p (e h j) r")
+                    .unsqueeze(1)
+                    .to_broadcast([P, 2, ROWS, 2]),
+                    op=MULT,
+                )
+                nc.gpsimd.tensor_tensor(
+                    out=result[:, :, t, :].rearrange("p (c h) d -> p c h d", c=2),
+                    in0=products[:, :, 0].rearrange("p c (h d) -> p c h d", d=HEAD),
+                    in1=products[:, :, 1].rearrange("p c (h d) -> p c h d", d=HEAD),
+                    op=ADD,
+                )
+            if t == TILES - 1:
+                heads = slice(half * PAIR_HEADS, (half + 1) * PAIR_HEADS)
+                nc.sync.dma_start(
+                    out=outputs[part][b, heads].rearrange("h (p t) d -> p h (t d)", t=TILES),
+                    in_=result[:].rearrange("p h t d -> p h (t d)"),
+                )
+
+        turn(("x", 0, 0), nc.vector.tensor_copy)
+        turn((Q, 0, 0))
+        quantise(("x", 0, 0))
+        turn((Q, 0, 1))
+        quantise((Q, 0, 0))
+        quantise((Q, 0, 1))
+        product(Q, 0, 0, 0)
+        turn(("x", 0, 1))
+        product(Q, 0, 0, 1)
+        quantise(("x", 0, 1))
+        turn(("x", 1, 0))
+        turn(("x", 1, 1))
+        product(Q, 0, 0, 2)
+        quantise(("x", 1, 0))
+        product(Q, 0, 0, 3)
+        quantise(("x", 1, 1))
+
+        steps = (
+            ((Q, 0), 1, None, ((KEY, 0), (V, 0))),
+            ((KEY, 0), 0, (V, 0), ((Q, 1),)),
+            ((KEY, 0), 1, (V, 0), ((V, 1),)),
+            ((Q, 1), 0, (V, 1), ((KEY, 1),)),
+            ((Q, 1), 1, (V, 1), ()),
+            ((KEY, 1), 0, None, ()),
+            ((KEY, 1), 1, None, ()),
+        )
+        for rotated, b, plain, ahead in steps:
+            for t in range(TILES):
+                if t % 2 == 0 and t // 2 < len(ahead):
+                    turn(ahead[t // 2] + (0,))
+                    turn(ahead[t // 2] + (1,))
+                product(*rotated, b, t)
+                if t // 2 < len(ahead):
+                    quantise(ahead[t // 2] + (t % 2,))
+                if plain:
+                    product(*plain, b, t)

@@ -60,7 +60,7 @@ def tile_bertselfattention_pa_kernel(
 
         for key in (("x", 0, 0), (Q, 0, 0), (Q, 0, 1), ("x", 0, 1), ("x", 1, 0), ("x", 1, 1)):
             load(key)
-        for part, half in ((KEY, 0), (V, 0), (Q, 1), (V, 1), (KEY, 1)):
+        for part, half in ((KEY, 0), (Q, 1), (KEY, 1), (V, 0), (V, 1)):
             load((part, half, 0))
             load((part, half, 1))
 
@@ -111,7 +111,7 @@ def tile_bertselfattention_pa_kernel(
 
         open_results = {}
 
-        def product(part, half, b, t):
+        def product(part, half, b, t, add=nc.gpsimd.tensor_tensor):
             x_codes, x_scales = ready[("x", b, t // 2)]
             sums = sum_banks.tile([P, 2, ROWS], F32, name="sums")
             for c in range(2):
@@ -147,7 +147,7 @@ def tile_bertselfattention_pa_kernel(
                     .to_broadcast([P, 2, ROWS, 2]),
                     op=MULT,
                 )
-                nc.gpsimd.tensor_tensor(
+                add(
                     out=result[:, :, t, :].rearrange("p (c h) d -> p c h d", c=2),
                     in0=products[:, :, 0].rearrange("p c (h d) -> p c h d", d=HEAD),
                     in1=products[:, :, 1].rearrange("p c (h d) -> p c h d", d=HEAD),
@@ -160,39 +160,40 @@ def tile_bertselfattention_pa_kernel(
                     in_=result[:].rearrange("p h t d -> p h (t d)"),
                 )
 
+        add = nc.vector.tensor_tensor
         turn(("x", 0, 0), nc.vector.tensor_copy)
         turn((Q, 0, 0))
         quantise(("x", 0, 0))
         turn((Q, 0, 1))
         quantise((Q, 0, 0))
         quantise((Q, 0, 1))
-        product(Q, 0, 0, 0)
+        product(Q, 0, 0, 0, add)
         turn(("x", 0, 1))
-        product(Q, 0, 0, 1)
+        product(Q, 0, 0, 1, add)
         quantise(("x", 0, 1))
         turn(("x", 1, 0))
         turn(("x", 1, 1))
-        product(Q, 0, 0, 2)
+        product(Q, 0, 0, 2, add)
         quantise(("x", 1, 0))
-        product(Q, 0, 0, 3)
+        product(Q, 0, 0, 3, add)
         quantise(("x", 1, 1))
+        for part, half in ((KEY, 0), (Q, 1), (KEY, 1), (V, 0), (V, 1)):
+            turn((part, half, 0))
+            turn((part, half, 1))
+            quantise((part, half, 0))
+            quantise((part, half, 1))
 
         steps = (
-            ((Q, 0), 1, None, ((KEY, 0), (V, 0))),
-            ((KEY, 0), 0, (V, 0), ((Q, 1),)),
-            ((KEY, 0), 1, (V, 0), ((V, 1),)),
-            ((Q, 1), 0, (V, 1), ((KEY, 1),)),
-            ((Q, 1), 1, (V, 1), ()),
-            ((KEY, 1), 0, None, ()),
-            ((KEY, 1), 1, None, ()),
+            ((Q, 0), 1, None),
+            ((KEY, 0), 0, (V, 0)),
+            ((KEY, 0), 1, (V, 0)),
+            ((Q, 1), 0, (V, 1)),
+            ((Q, 1), 1, (V, 1)),
+            ((KEY, 1), 0, None),
+            ((KEY, 1), 1, None),
         )
-        for rotated, b, plain, ahead in steps:
+        for rotated, b, plain in steps:
             for t in range(TILES):
-                if t % 2 == 0 and t // 2 < len(ahead):
-                    turn(ahead[t // 2] + (0,))
-                    turn(ahead[t // 2] + (1,))
                 product(*rotated, b, t)
-                if t // 2 < len(ahead):
-                    quantise(ahead[t // 2] + (t % 2,))
                 if plain:
                     product(*plain, b, t)

@@ -110,8 +110,9 @@ def tile_bertselfattention_pa_kernel(
             ready[key] = (codes, scales)
 
         open_results = {}
+        open_products = {}
 
-        def product(part, half, b, t, add=nc.gpsimd.tensor_tensor):
+        def multiply(part, half, b, t):
             x_codes, x_scales = ready[("x", b, t // 2)]
             sums = sum_banks.tile([P, 2, ROWS], F32, name="sums")
             for c in range(2):
@@ -130,53 +131,70 @@ def tile_bertselfattention_pa_kernel(
                     )
             if t == 0:
                 open_results[(part, half, b)] = results.tile([P, PAIR_HEADS, TILES, HEAD], F32, name="result")
-            result = open_results[(part, half, b)]
-            if part == V:
-                nc.scalar.copy(
-                    out=result[:, :, t, :].rearrange("p (c h) (j r) -> p c h j r", c=2, r=2),
-                    in_=sums[:].rearrange("p c (r h j) -> p c h j r", r=2, h=CHUNK_HEADS),
-                )
-            else:
-                products = work.tile([P, 2, 2, CHUNK_HEADS * HEAD], F32, name="products")
-                nc.vector.tensor_tensor(
-                    out=products[:].rearrange("p c e (m r) -> p c (e m) r", r=2),
-                    in0=sums[:].unsqueeze(3).to_broadcast([P, 2, ROWS, 2]),
-                    in1=factors[:, t]
-                    .rearrange("p e h j r -> p (e h j) r")
-                    .unsqueeze(1)
-                    .to_broadcast([P, 2, ROWS, 2]),
-                    op=MULT,
-                )
-                add(
-                    out=result[:, :, t, :].rearrange("p (c h) d -> p c h d", c=2),
-                    in0=products[:, :, 0].rearrange("p c (h d) -> p c h d", d=HEAD),
-                    in1=products[:, :, 1].rearrange("p c (h d) -> p c h d", d=HEAD),
-                    op=ADD,
-                )
-            if t == TILES - 1:
-                heads = slice(half * PAIR_HEADS, (half + 1) * PAIR_HEADS)
-                nc.sync.dma_start(
-                    out=outputs[part][b, heads].rearrange("h (p t) d -> p h (t d)", t=TILES),
-                    in_=result[:].rearrange("p h t d -> p h (t d)"),
-                )
+            return sums
 
-        add = nc.vector.tensor_tensor
+        def store(part, half, b):
+            heads = slice(half * PAIR_HEADS, (half + 1) * PAIR_HEADS)
+            nc.sync.dma_start(
+                out=outputs[part][b, heads].rearrange("h (p t) d -> p h (t d)", t=TILES),
+                in_=open_results[(part, half, b)][:].rearrange("p h t d -> p h (t d)"),
+            )
+
+        def plain(half, b, t):
+            sums = multiply(V, half, b, t)
+            nc.scalar.copy(
+                out=open_results[(V, half, b)][:, :, t, :].rearrange("p (c h) (j r) -> p c h j r", c=2, r=2),
+                in_=sums[:].rearrange("p c (r h j) -> p c h j r", r=2, h=CHUNK_HEADS),
+            )
+            if t == TILES - 1:
+                store(V, half, b)
+
+        def rotate(part, half, b, t):
+            sums = multiply(part, half, b, t)
+            if t % 2 == 0:
+                open_products[(part, half, b, t)] = work.tile(
+                    [P, 2, 2, 2, CHUNK_HEADS * HEAD], F32, name="products"
+                )
+            nc.vector.tensor_tensor(
+                out=open_products[(part, half, b, t - t % 2)][:, t % 2].rearrange("p c e (m r) -> p c (e m) r", r=2),
+                in0=sums[:].unsqueeze(3).to_broadcast([P, 2, ROWS, 2]),
+                in1=factors[:, t]
+                .rearrange("p e h j r -> p (e h j) r")
+                .unsqueeze(1)
+                .to_broadcast([P, 2, ROWS, 2]),
+                op=MULT,
+            )
+
+        def add_terms(part, half, b, t, add):
+            terms = open_products[(part, half, b, t)][:].rearrange("p t c e (h d) -> p t c e h d", d=HEAD)
+            result = open_results[(part, half, b)]
+            add(
+                out=result[:, :, t : t + 2, :].rearrange("p (c h) t d -> p t c h d", c=2),
+                in0=terms[:, :, :, 0],
+                in1=terms[:, :, :, 1],
+                op=ADD,
+            )
+            if t + 2 == TILES:
+                store(part, half, b)
+
         turn(("x", 0, 0), nc.vector.tensor_copy)
         turn((Q, 0, 0))
         quantise(("x", 0, 0))
         turn((Q, 0, 1))
         quantise((Q, 0, 0))
         quantise((Q, 0, 1))
-        product(Q, 0, 0, 0, add)
+        rotate(Q, 0, 0, 0)
         turn(("x", 0, 1))
-        product(Q, 0, 0, 1, add)
+        rotate(Q, 0, 0, 1)
         quantise(("x", 0, 1))
         turn(("x", 1, 0))
         turn(("x", 1, 1))
-        product(Q, 0, 0, 2, add)
+        add_terms(Q, 0, 0, 0, nc.vector.tensor_tensor)
+        rotate(Q, 0, 0, 2)
         quantise(("x", 1, 0))
-        product(Q, 0, 0, 3, add)
+        rotate(Q, 0, 0, 3)
         quantise(("x", 1, 1))
+        add_terms(Q, 0, 0, 2, nc.vector.tensor_tensor)
         for part, half in ((KEY, 0), (Q, 1), (KEY, 1), (V, 0), (V, 1)):
             turn((part, half, 0))
             turn((part, half, 1))
@@ -185,15 +203,18 @@ def tile_bertselfattention_pa_kernel(
 
         steps = (
             ((Q, 0), 1, None),
-            ((KEY, 0), 0, (V, 0)),
-            ((KEY, 0), 1, (V, 0)),
-            ((Q, 1), 0, (V, 1)),
-            ((Q, 1), 1, (V, 1)),
+            ((KEY, 0), 0, (0, 0)),
+            ((KEY, 0), 1, (0, 1)),
+            ((Q, 1), 0, (1, 0)),
+            ((Q, 1), 1, (1, 1)),
             ((KEY, 1), 0, None),
             ((KEY, 1), 1, None),
         )
-        for rotated, b, plain in steps:
+        for rotated, b, v_tiles in steps:
             for t in range(TILES):
-                product(*rotated, b, t)
-                if plain:
-                    product(*plain, b, t)
+                rotate(*rotated, b, t)
+                if t % 2 == 1:
+                    last = rotated == (KEY, 1) and b == BATCH - 1 and t == TILES - 1
+                    add_terms(*rotated, b, t - 1, nc.vector.tensor_tensor if last else nc.gpsimd.tensor_tensor)
+                if v_tiles:
+                    plain(*v_tiles, t)

@@ -72,7 +72,7 @@ def tile_bertselfattention_pa_kernel(
         identity = keep.tile([P, P], F32, name="identity")
         make_identity(nc, identity[:])
 
-        factors = keep.tile([P, TILES, 2, CHUNK_HEADS, PAIRS, 2], F32, name="factors")
+        factors = keep.tile([P, TILES, 2, CHUNK_HEADS, PAIRS, 2], BF16, name="factors")
         rotation = ((0, 0, cos_rows, 1.0), (0, 1, sin_rows, -1.0), (1, 0, sin_rows, 1.0), (1, 1, cos_rows, 1.0))
         for r, e, rows, sign in rotation:
             nc.gpsimd.tensor_scalar(
@@ -84,13 +84,13 @@ def tile_bertselfattention_pa_kernel(
                 op1=ADD,
             )
 
-        grouped_chunks = {}
         ready = {}
 
-        def turn(key, empty=nc.scalar.copy):
+        def turn(key, empty=nc.scalar.copy, grouped=None):
             words = chunk_rows[key][:].bitcast(F32)
-            grouped = stage.tile([P, CHUNK_COLS * 4], BF16, align_bytes=64, name="grouped")
-            grouped_words = grouped[:].bitcast(F32).rearrange("p (i c u) -> p i c u", c=ROWS, u=2)
+            if grouped is None:
+                grouped = stage.tile([P, CHUNK_COLS * 4], BF16, align_bytes=64, name="grouped")[:]
+            grouped_words = grouped.bitcast(F32).rearrange("p (i c u) -> p i c u", c=ROWS, u=2)
             for i in range(2):
                 turned = turned_banks.tile([P, 2, ROWS], F32, name="turned")
                 for c in range(2):
@@ -101,25 +101,31 @@ def tile_bertselfattention_pa_kernel(
                             turned[:, u, c * P : (c + 1) * P], words[:, start : start + P], identity[:]
                         )
                 empty(out=grouped_words[:, i], in_=turned[:].rearrange("p u c -> p c u"))
-            grouped_chunks[key] = grouped
+            return grouped
 
-        def quantise(key):
-            codes = keep.tile([P, CHUNK_COLS], U32, align_bytes=64, name="codes_%s%d%d" % key)
-            scales = keep.tile([P, CHUNK_COLS], U8, align_bytes=64, name="scales_%s%d%d" % key)
-            nc.vector.quantize_mx(out=codes[:].bitcast(FP8X4), scales=scales[:], in_=grouped_chunks[key][:])
-            ready[key] = (codes, scales)
+        def quantise(keys, grouped):
+            name = "%s%d%d" % keys[0]
+            codes = keep.tile([P, len(keys) * CHUNK_COLS], U32, align_bytes=64, name="codes_" + name)
+            scales = keep.tile([P, len(keys) * CHUNK_COLS], U8, align_bytes=64, name="scales_" + name)
+            nc.vector.quantize_mx(out=codes[:].bitcast(FP8X4), scales=scales[:], in_=grouped)
+            for n, key in enumerate(keys):
+                ready[key] = (codes, scales, n * CHUNK_COLS)
 
         open_results = {}
         open_products = {}
 
         def multiply(part, half, b, t):
-            x_codes, x_scales = ready[("x", b, t // 2)]
-            sums = sum_banks.tile([P, 2, ROWS], F32, name="sums")
+            x_codes, x_scales, x_first = ready[("x", b, t // 2)]
+            if part == V:
+                sums = turned_banks.tile([P, 2, ROWS], F32, name="turned")
+            else:
+                sums = sum_banks.tile([P, 2, ROWS], F32, name="sums")
             for c in range(2):
-                w_codes, w_scales = ready[(part, half, c)]
+                w_codes, w_scales, w_first = ready[(part, half, c)]
                 for g in range(PASSES):
-                    tokens = slice(((t % 2) * PASSES + g) * P, ((t % 2) * PASSES + g + 1) * P)
-                    columns = slice(g * ROWS, (g + 1) * ROWS)
+                    token = x_first + ((t % 2) * PASSES + g) * P
+                    tokens = slice(token, token + P)
+                    columns = slice(w_first + g * ROWS, w_first + (g + 1) * ROWS)
                     nc.tensor.matmul_mx(
                         out=sums[:, c],
                         lhsT=x_codes[:, tokens].bitcast(FP8X4),
@@ -165,41 +171,44 @@ def tile_bertselfattention_pa_kernel(
                 op=MULT,
             )
 
-        def add_terms(part, half, b, t, add):
-            terms = open_products[(part, half, b, t)][:].rearrange("p t c e (h d) -> p t c e h d", d=HEAD)
+        def add_terms(part, half, b, t, tiles, add):
+            i = t % 2
+            products = open_products[(part, half, b, t - i)]
+            terms = products[:, i : i + tiles].rearrange("p t c e (h d) -> p t c e h d", d=HEAD)
             result = open_results[(part, half, b)]
             add(
-                out=result[:, :, t : t + 2, :].rearrange("p (c h) t d -> p t c h d", c=2),
+                out=result[:, :, t : t + tiles, :].rearrange("p (c h) t d -> p t c h d", c=2),
                 in0=terms[:, :, :, 0],
                 in1=terms[:, :, :, 1],
                 op=ADD,
             )
-            if t + 2 == TILES:
-                store(part, half, b)
 
-        turn(("x", 0, 0), nc.vector.tensor_copy)
-        turn((Q, 0, 0))
-        quantise(("x", 0, 0))
-        turn((Q, 0, 1))
-        quantise((Q, 0, 0))
-        quantise((Q, 0, 1))
+        x00, x01, x10, x11 = ("x", 0, 0), ("x", 0, 1), ("x", 1, 0), ("x", 1, 1)
+        q0, q1 = (Q, 0, 0), (Q, 0, 1)
+        grouped_x = turn(x00, nc.vector.tensor_copy)
+        grouped_q0 = turn(q0)
+        quantise([x00], grouped_x)
+        grouped_q1 = turn(q1, nc.vector.tensor_copy)
+        quantise([q0], grouped_q0)
+        quantise([q1], grouped_q1)
         rotate(Q, 0, 0, 0)
-        turn(("x", 0, 1))
+        grouped_x = turn(x01)
         rotate(Q, 0, 0, 1)
-        quantise(("x", 0, 1))
-        turn(("x", 1, 0))
-        turn(("x", 1, 1))
-        add_terms(Q, 0, 0, 0, nc.vector.tensor_tensor)
+        quantise([x01], grouped_x)
+        both = stage.tile([P, 2, CHUNK_COLS * 4], BF16, align_bytes=64, name="grouped_pair")
+        turn(x10, grouped=both[:, 0])
+        turn(x11, grouped=both[:, 1])
+        add_terms(Q, 0, 0, 0, 2, nc.vector.tensor_tensor)
         rotate(Q, 0, 0, 2)
-        quantise(("x", 1, 0))
         rotate(Q, 0, 0, 3)
-        quantise(("x", 1, 1))
-        add_terms(Q, 0, 0, 2, nc.vector.tensor_tensor)
+        quantise([x10, x11], both[:].rearrange("p n c -> p (n c)"))
+        add_terms(Q, 0, 0, 2, 2, nc.vector.tensor_tensor)
+        store(Q, 0, 0)
         for part, half in ((KEY, 0), (Q, 1), (KEY, 1), (V, 0), (V, 1)):
-            turn((part, half, 0))
-            turn((part, half, 1))
-            quantise((part, half, 0))
-            quantise((part, half, 1))
+            both = stage.tile([P, 2, CHUNK_COLS * 4], BF16, align_bytes=64, name="grouped_pair")
+            for c in range(2):
+                turn((part, half, c), grouped=both[:, c])
+            quantise([(part, half, 0), (part, half, 1)], both[:].rearrange("p n c -> p (n c)"))
 
         steps = (
             ((Q, 0), 1, None),
@@ -211,10 +220,12 @@ def tile_bertselfattention_pa_kernel(
             ((KEY, 1), 1, None),
         )
         for rotated, b, v_tiles in steps:
+            last = (rotated, b) == ((KEY, 1), 1)
             for t in range(TILES):
                 rotate(*rotated, b, t)
-                if t % 2 == 1:
-                    last = rotated == (KEY, 1) and b == BATCH - 1 and t == TILES - 1
-                    add_terms(*rotated, b, t - 1, nc.vector.tensor_tensor if last else nc.gpsimd.tensor_tensor)
                 if v_tiles:
                     plain(*v_tiles, t)
+                if t % 2 == 1:
+                    on_vector = last and t == TILES - 1
+                    add_terms(*rotated, b, t - 1, 2, nc.vector.tensor_tensor if on_vector else nc.gpsimd.tensor_tensor)
+            store(*rotated, b)

@@ -139,11 +139,13 @@ def tile_bertselfattention_pa_kernel(
                 open_results[(part, half, b)] = results.tile([P, PAIR_HEADS, TILES, HEAD], F32, name="result")
             return sums
 
-        def store(part, half, b):
-            heads = slice(half * PAIR_HEADS, (half + 1) * PAIR_HEADS)
+        def store(part, half, b, heads=slice(0, PAIR_HEADS)):
+            first = half * PAIR_HEADS
             nc.sync.dma_start(
-                out=outputs[part][b, heads].rearrange("h (p t) d -> p h (t d)", t=TILES),
-                in_=open_results[(part, half, b)][:].rearrange("p h t d -> p h (t d)"),
+                out=outputs[part][b, first + heads.start : first + heads.stop].rearrange(
+                    "h (p t) d -> p h (t d)", t=TILES
+                ),
+                in_=open_results[(part, half, b)][:, heads].rearrange("p h t d -> p h (t d)"),
             )
 
         def plain(half, b, t):
@@ -171,16 +173,26 @@ def tile_bertselfattention_pa_kernel(
                 op=MULT,
             )
 
-        def add_terms(part, half, b, t, tiles, add):
+        def add_terms(part, half, b, t, tiles, add, chunks=slice(0, 2)):
             i = t % 2
             products = open_products[(part, half, b, t - i)]
-            terms = products[:, i : i + tiles].rearrange("p t c e (h d) -> p t c e h d", d=HEAD)
-            result = open_results[(part, half, b)]
+            terms = products[:, i : i + tiles, chunks].rearrange("p t c e (h d) -> p t c e h d", d=HEAD)
+            result = open_results[(part, half, b)][:, chunks.start * CHUNK_HEADS : chunks.stop * CHUNK_HEADS]
             add(
-                out=result[:, :, t : t + tiles, :].rearrange("p (c h) t d -> p t c h d", c=2),
+                out=result[:, :, t : t + tiles, :].rearrange("p (c h) t d -> p t c h d", h=CHUNK_HEADS),
                 in0=terms[:, :, :, 0],
                 in1=terms[:, :, :, 1],
                 op=ADD,
+            )
+
+        def add_on_tensor(part, half, b, t):
+            terms = open_products[(part, half, b, t - t % 2)][:, t % 2]
+            total = turned_banks.tile([P, 2, ROWS], F32, name="turned")
+            for e in range(2):
+                nc.tensor.matmul(total[:], lhsT=identity[:], rhs=terms[:, :, e], start=(e == 0), stop=(e == 1))
+            nc.scalar.copy(
+                out=open_results[(part, half, b)][:, :, t, :],
+                in_=total[:].rearrange("p c (h d) -> p (c h) d", d=HEAD),
             )
 
         x00, x01, x10, x11 = ("x", 0, 0), ("x", 0, 1), ("x", 1, 0), ("x", 1, 1)
@@ -188,7 +200,7 @@ def tile_bertselfattention_pa_kernel(
         grouped_x = turn(x00, nc.vector.tensor_copy)
         grouped_q0 = turn(q0)
         quantise([x00], grouped_x)
-        grouped_q1 = turn(q1, nc.vector.tensor_copy)
+        grouped_q1 = turn(q1)
         quantise([q0], grouped_q0)
         quantise([q1], grouped_q1)
         rotate(Q, 0, 0, 0)
@@ -204,28 +216,48 @@ def tile_bertselfattention_pa_kernel(
         quantise([x10, x11], both[:].rearrange("p n c -> p (n c)"))
         add_terms(Q, 0, 0, 2, 2, nc.vector.tensor_tensor)
         store(Q, 0, 0)
-        for part, half in ((KEY, 0), (Q, 1), (KEY, 1), (V, 0), (V, 1)):
+
+        def turn_pair(part, half):
             both = stage.tile([P, 2, CHUNK_COLS * 4], BF16, align_bytes=64, name="grouped_pair")
             for c in range(2):
                 turn((part, half, c), grouped=both[:, c])
-            quantise([(part, half, 0), (part, half, 1)], both[:].rearrange("p n c -> p (n c)"))
+            return both[:].rearrange("p n c -> p (n c)")
 
+        def quantise_pair(part, half, grouped):
+            quantise([(part, half, 0), (part, half, 1)], grouped)
+
+        for part, half in ((KEY, 0), (Q, 1), (KEY, 1)):
+            quantise_pair(part, half, turn_pair(part, half))
+
+        for t in range(TILES):
+            rotate(Q, 0, 1, t)
+            add_terms(Q, 0, 1, t, 1, nc.gpsimd.tensor_tensor)
+            if t % 2 == 0:
+                grouped_v = turn_pair(V, t // 2)
+            else:
+                quantise_pair(V, t // 2, grouped_v)
+        store(Q, 0, 1)
         steps = (
-            ((Q, 0), 1, None),
-            ((KEY, 0), 0, (0, 0)),
-            ((KEY, 0), 1, (0, 1)),
-            ((Q, 1), 0, (1, 0)),
-            ((Q, 1), 1, (1, 1)),
-            ((KEY, 1), 0, None),
-            ((KEY, 1), 1, None),
+            ((KEY, 0), 0, None),
+            ((KEY, 0), 1, (0, 0)),
+            ((Q, 1), 0, (0, 1)),
+            ((Q, 1), 1, (1, 0)),
+            ((KEY, 1), 0, (1, 1)),
         )
         for rotated, b, v_tiles in steps:
-            last = (rotated, b) == ((KEY, 1), 1)
             for t in range(TILES):
                 rotate(*rotated, b, t)
+                if t % 2 == 1:
+                    add_terms(*rotated, b, t - 1, 2, nc.gpsimd.tensor_tensor)
                 if v_tiles:
                     plain(*v_tiles, t)
-                if t % 2 == 1:
-                    on_vector = last and t == TILES - 1
-                    add_terms(*rotated, b, t - 1, 2, nc.vector.tensor_tensor if on_vector else nc.gpsimd.tensor_tensor)
             store(*rotated, b)
+
+        last = (KEY, 1, 1)
+        for t in range(TILES):
+            rotate(*last, t)
+        for t in range(2):
+            add_on_tensor(*last, t)
+        for c in range(2):
+            add_terms(*last, 2, 2, nc.vector.tensor_tensor, slice(c, c + 1))
+            store(*last, slice(c * CHUNK_HEADS, (c + 1) * CHUNK_HEADS))

@@ -244,11 +244,12 @@ def tile_bertselfattention_pa_kernel(
             ((Q, 1), 1, (1, 0)),
             ((KEY, 1), 0, (1, 1)),
         )
-        for rotated, b, v_tiles in steps:
+        for n, (rotated, b, v_tiles) in enumerate(steps):
             for t in range(TILES):
                 rotate(*rotated, b, t)
                 if t % 2 == 1:
-                    add_terms(*rotated, b, t - 1, 2, nc.gpsimd.tensor_tensor)
+                    on_vector = n % 2 == 1 and t == 1
+                    add_terms(*rotated, b, t - 1, 2, nc.vector.tensor_tensor if on_vector else nc.gpsimd.tensor_tensor)
                 if v_tiles:
                     plain(*v_tiles, t)
             store(*rotated, b)

from contextlib import ExitStack

import concourse.mybir as mybir
from concourse.masks import make_identity

BF16 = mybir.dt.bfloat16
F32 = mybir.dt.float32
U32 = mybir.dt.uint32
U8 = mybir.dt.uint8
FP8X4 = mybir.dt.float8_e4m3fn_x4
MULT = mybir.AluOpType.mult
ADD = mybir.AluOpType.add

P = 128
BATCH = 2
POSITIONS = 512
K = 1024
HEAD = 64
PAIRS = HEAD // 2
TILES = POSITIONS // P
PASSES = K // (P * 4)
ROWS = 2 * P
ROW_WORDS = K // 2
PASS_WORDS = ROW_WORDS // PASSES
CHUNK_COLS = PASSES * ROWS
CHUNK_HEADS = ROWS // HEAD
PAIR_HEADS = 2 * CHUNK_HEADS
N = 2 * ROWS
Q, KEY, V = 0, 1, 2

FLOPS = 2 * BATCH * POSITIONS * K * 3072


def tile_bertselfattention_pa_kernel(
    tc, hidden_states, w_qkv, freqs_cos, freqs_sin, out_0, out_1, out_2
):
    nc = tc.nc
    outputs = (out_0, out_1, out_2)

    with ExitStack() as stack:
        keep = stack.enter_context(tc.tile_pool(name="keep", bufs=1))
        stage = stack.enter_context(tc.tile_pool(name="stage", bufs=4))
        work = stack.enter_context(tc.tile_pool(name="work", bufs=4))
        results = stack.enter_context(tc.tile_pool(name="results", bufs=6))
        turned_banks = stack.enter_context(tc.psum_pool(name="turned_banks", bufs=4))
        sum_banks = stack.enter_context(tc.psum_pool(name="sum_banks", bufs=4))

        chunk_rows = {}

        def load(key):
            rows = keep.tile([P, 2 * K], BF16, name="rows_%s%d%d" % key)
            name, i, c = key
            if name == "x":
                source = hidden_states[i].rearrange("(p t) k -> p t k", t=TILES)[:, 2 * c : 2 * c + 2, :]
            else:
                first = name * 1024 + (2 * i + c) * ROWS
                source = w_qkv[first : first + ROWS, :].rearrange("(p e) k -> p e k", e=2)
            nc.sync.dma_start(out=rows[:].rearrange("p (e k) -> p e k", e=2), in_=source)
            chunk_rows[key] = rows

        for key in (("x", 0, 0), (Q, 0, 0), (Q, 0, 1), ("x", 0, 1), ("x", 1, 0), ("x", 1, 1)):
            load(key)
        for part, half in ((KEY, 0), (Q, 1), (KEY, 1), (V, 0), (V, 1)):
            load((part, half, 0))
            load((part, half, 1))

        cos_rows = keep.tile([P, TILES, PAIRS], BF16, name="cos_rows")
        sin_rows = keep.tile([P, TILES, PAIRS], BF16, name="sin_rows")
        nc.scalar.dma_start(out=cos_rows[:], in_=freqs_cos.rearrange("(p t) j -> p t j", t=TILES))
        nc.scalar.dma_start(out=sin_rows[:], in_=freqs_sin.rearrange("(p t) j -> p t j", t=TILES))

        identity = keep.tile([P, P], F32, name="identity")
        make_identity(nc, identity[:])

        factors = keep.tile([P, TILES, 2, CHUNK_HEADS, PAIRS, 2], BF16, name="factors")
        rotation = ((0, 0, cos_rows, 1.0), (0, 1, sin_rows, -1.0), (1, 0, sin_rows, 1.0), (1, 1, cos_rows, 1.0))
        for r, e, rows, sign in rotation:
            nc.gpsimd.tensor_scalar(
                out=factors[:, :, e, :, :, r],
                in0=rows[:].unsqueeze(2).to_broadcast([P, TILES, CHUNK_HEADS, PAIRS]),
                scalar1=sign,
                scalar2=0.0,
                op0=MULT,
                op1=ADD,
            )

        ready = {}

        def turn(key, empty=nc.scalar.copy, grouped=None):
            words = chunk_rows[key][:].bitcast(F32)
            if grouped is None:
                grouped = stage.tile([P, CHUNK_COLS * 4], BF16, align_bytes=64, name="grouped")[:]
            grouped_words = grouped.bitcast(F32).rearrange("p (i c u) -> p i c u", c=ROWS, u=2)
            for i in range(2):
                turned = turned_banks.tile([P, 2, ROWS], F32, name="turned")
                for c in range(2):
                    row, g = (i, c) if key[0] == "x" else (c, i)
                    for u in range(2):
                        start = row * ROW_WORDS + g * PASS_WORDS + u * P
                        nc.tensor.transpose(
                            turned[:, u, c * P : (c + 1) * P], words[:, start : start + P], identity[:]
                        )
                empty(out=grouped_words[:, i], in_=turned[:].rearrange("p u c -> p c u"))
            return grouped

        def quantise(keys, grouped):
            name = "%s%d%d" % keys[0]
            codes = keep.tile([P, len(keys) * CHUNK_COLS], U32, align_bytes=64, name="codes_" + name)
            scales = keep.tile([P, len(keys) * CHUNK_COLS], U8, align_bytes=64, name="scales_" + name)
            nc.vector.quantize_mx(out=codes[:].bitcast(FP8X4), scales=scales[:], in_=grouped)
            for n, key in enumerate(keys):
                ready[key] = (codes, scales, n * CHUNK_COLS)

        open_results = {}
        open_products = {}

        def multiply(part, half, b, t):
            x_codes, x_scales, x_first = ready[("x", b, t // 2)]
            if part == V:
                sums = turned_banks.tile([P, 2, ROWS], F32, name="turned")
            else:
                sums = sum_banks.tile([P, 2, ROWS], F32, name="sums")
            for c in range(2):
                w_codes, w_scales, w_first = ready[(part, half, c)]
                for g in range(PASSES):
                    token = x_first + ((t % 2) * PASSES + g) * P
                    tokens = slice(token, token + P)
                    columns = slice(w_first + g * ROWS, w_first + (g + 1) * ROWS)
                    nc.tensor.matmul_mx(
                        out=sums[:, c],
                        lhsT=x_codes[:, tokens].bitcast(FP8X4),
                        lhsT_scale=x_scales[:, tokens],
                        rhs=w_codes[:, columns].bitcast(FP8X4),
                        rhs_scale=w_scales[:, columns],
                        start=(g == 0),
                        stop=(g == PASSES - 1),
                    )
            if t == 0:
                open_results[(part, half, b)] = results.tile([P, PAIR_HEADS, TILES, HEAD], F32, name="result")
            return sums

        def store(part, half, b, heads=slice(0, PAIR_HEADS)):
            first = half * PAIR_HEADS
            nc.sync.dma_start(
                out=outputs[part][b, first + heads.start : first + heads.stop].rearrange(
                    "h (p t) d -> p h (t d)", t=TILES
                ),
                in_=open_results[(part, half, b)][:, heads].rearrange("p h t d -> p h (t d)"),
            )

        def plain(half, b, t):
            sums = multiply(V, half, b, t)
            nc.scalar.copy(
                out=open_results[(V, half, b)][:, :, t, :].rearrange("p (c h) (j r) -> p c h j r", c=2, r=2),
                in_=sums[:].rearrange("p c (r h j) -> p c h j r", r=2, h=CHUNK_HEADS),
            )
            if t == TILES - 1:
                store(V, half, b)

        def rotate(part, half, b, t):
            sums = multiply(part, half, b, t)
            if t % 2 == 0:
                open_products[(part, half, b, t)] = work.tile(
                    [P, 2, 2, 2, CHUNK_HEADS * HEAD], F32, name="products"
                )
            nc.vector.tensor_tensor(
                out=open_products[(part, half, b, t - t % 2)][:, t % 2].rearrange("p c e (m r) -> p c (e m) r", r=2),
                in0=sums[:].unsqueeze(3).to_broadcast([P, 2, ROWS, 2]),
                in1=factors[:, t]
                .rearrange("p e h j r -> p (e h j) r")
                .unsqueeze(1)
                .to_broadcast([P, 2, ROWS, 2]),
                op=MULT,
            )

        def add_terms(part, half, b, t, tiles, add, chunks=slice(0, 2)):
            i = t % 2
            products = open_products[(part, half, b, t - i)]
            terms = products[:, i : i + tiles, chunks].rearrange("p t c e (h d) -> p t c e h d", d=HEAD)
            result = open_results[(part, half, b)][:, chunks.start * CHUNK_HEADS : chunks.stop * CHUNK_HEADS]
            add(
                out=result[:, :, t : t + tiles, :].rearrange("p (c h) t d -> p t c h d", h=CHUNK_HEADS),
                in0=terms[:, :, :, 0],
                in1=terms[:, :, :, 1],
                op=ADD,
            )

        def add_on_tensor(part, half, b, t):
            terms = open_products[(part, half, b, t - t % 2)][:, t % 2]
            total = turned_banks.tile([P, 2, ROWS], F32, name="turned")
            for e in range(2):
                nc.tensor.matmul(total[:], lhsT=identity[:], rhs=terms[:, :, e], start=(e == 0), stop=(e == 1))
            nc.scalar.copy(
                out=open_results[(part, half, b)][:, :, t, :],
                in_=total[:].rearrange("p c (h d) -> p (c h) d", d=HEAD),
            )

        x00, x01, x10, x11 = ("x", 0, 0), ("x", 0, 1), ("x", 1, 0), ("x", 1, 1)
        q0, q1 = (Q, 0, 0), (Q, 0, 1)
        grouped_x = turn(x00, nc.vector.tensor_copy)
        grouped_q0 = turn(q0)
        quantise([x00], grouped_x)
        grouped_q1 = turn(q1)
        quantise([q0], grouped_q0)
        quantise([q1], grouped_q1)
        rotate(Q, 0, 0, 0)
        grouped_x = turn(x01)
        rotate(Q, 0, 0, 1)
        quantise([x01], grouped_x)
        both = stage.tile([P, 2, CHUNK_COLS * 4], BF16, align_bytes=64, name="grouped_pair")
        turn(x10, grouped=both[:, 0])
        turn(x11, grouped=both[:, 1])
        add_terms(Q, 0, 0, 0, 2, nc.vector.tensor_tensor)
        rotate(Q, 0, 0, 2)
        rotate(Q, 0, 0, 3)
        quantise([x10, x11], both[:].rearrange("p n c -> p (n c)"))
        add_terms(Q, 0, 0, 2, 2, nc.vector.tensor_tensor)
        store(Q, 0, 0)

        def turn_pair(part, half):
            both = stage.tile([P, 2, CHUNK_COLS * 4], BF16, align_bytes=64, name="grouped_pair")
            for c in range(2):
                turn((part, half, c), grouped=both[:, c])
            return both[:].rearrange("p n c -> p (n c)")

        def quantise_pair(part, half, grouped):
            quantise([(part, half, 0), (part, half, 1)], grouped)

        for part, half in ((KEY, 0), (Q, 1), (KEY, 1)):
            quantise_pair(part, half, turn_pair(part, half))

        for t in range(TILES):
            rotate(Q, 0, 1, t)
            add_terms(Q, 0, 1, t, 1, nc.gpsimd.tensor_tensor)
            if t % 2 == 0:
                grouped_v = turn_pair(V, t // 2)
            else:
                quantise_pair(V, t // 2, grouped_v)
        store(Q, 0, 1)
        steps = (
            ((KEY, 0), 0, None),
            ((KEY, 0), 1, (0, 0)),
            ((Q, 1), 0, (0, 1)),
            ((Q, 1), 1, (1, 0)),
            ((KEY, 1), 0, (1, 1)),
        )
        for n, (rotated, b, v_tiles) in enumerate(steps):
            for t in range(TILES):
                rotate(*rotated, b, t)
                if t % 2 == 1:
                    on_vector = n % 2 == 1 and t == 1
                    add_terms(*rotated, b, t - 1, 2, nc.vector.tensor_tensor if on_vector else nc.gpsimd.tensor_tensor)
                if v_tiles:
                    plain(*v_tiles, t)
            store(*rotated, b)

        last = (KEY, 1, 1)
        for t in range(TILES):
            rotate(*last, t)
        for t in range(2):
            add_on_tensor(*last, t)
        for c in range(2):
            add_terms(*last, 2, 2, nc.vector.tensor_tensor, slice(c, c + 1))
            store(*last, slice(c * CHUNK_HEADS, (c + 1) * CHUNK_HEADS))
